import numpy as np
import ml_dtypes

BF16 = ml_dtypes.bfloat16


def bf(x):
    return np.asarray(x, np.float32).astype(BF16)


def f32(x):
    return np.asarray(x, np.float32)


def f64(x):
    return np.asarray(x).astype(np.float64)


def striped(idx):
    return np.tile(idx.reshape(-1, 16).T, (8, 1))


S, D, M, N, E = 512, 128, 512, 256, 64


def setup_inputs():
    table = bf(np.random.standard_normal((S, D)))
    w = bf(np.concatenate([0.5 * np.random.standard_normal((D, M - D)) / np.sqrt(D), np.eye(D)], axis=1))
    values = f32(np.random.standard_normal((1, N)))
    times = f32(np.random.uniform(size=(1, N)))
    a1 = f32(np.random.standard_normal((D, 1)))
    c1 = f32(0.1 * np.random.standard_normal((D, 1)))
    cw2 = bf(1.5 * np.random.standard_normal((D, D)) / np.sqrt(D))
    idx = np.random.permutation(np.tile(np.arange(S), 2))[:N]
    return {'table': table, 'w': w, 'values': values, 'times': times, 'a1': a1, 'c1': c1, 'cw2': cw2, 'offs': striped(idx)}


def reference(table, w, values, times, a1, c1, cw2, offs):
    idx = offs[:16].T.reshape(-1)
    u = np.concatenate([np.repeat(f64(values), E, axis=0), np.repeat(f64(times), D - E, axis=0)], axis=0)
    h = np.tanh(f64(a1) * u + f64(c1))
    cont = f64(cw2).T @ h
    return f64(w).T @ f64(table)[idx].T + f64(w).T @ cont

@@ -1,0 +1,68 @@
+import concourse.masks as masks
+import concourse.mybir as mybir
+
+P = 128
+S, D, M, N, E = 512, 128, 512, 256, 64
+BF16, F32, U16 = mybir.dt.bfloat16, mybir.dt.float32, mybir.dt.uint16
+TANH = mybir.ActivationFunctionType.Tanh
+
+FLOPS = 2 * D * M * N * 2 + 2 * D * D * N
+
+
+def tile_strats_kernel(tc, table, w, values, times, a1, c1, cw2, offs, out):
+    nc = tc.nc
+    with (
+        tc.tile_pool(name="held", bufs=1) as held,
+        tc.psum_pool(name="psum", bufs=1) as psum,
+    ):
+        offsets = held.tile([P, N // 16], U16, name="offsets")
+        nc.sync.dma_start(offsets[:], offs)
+
+        table_rows = held.tile([P, S // P, D], BF16, name="table_rows")
+        nc.sync.dma_start(table_rows[:], table.rearrange("(c p) d -> p c d", p=P))
+
+        u = held.tile([P, N], F32, name="u")
+        nc.scalar.dma_start(u[0:E, :], values.broadcast_to([E, N]))
+        nc.scalar.dma_start(u[E:P, :], times.broadcast_to([P - E, N]))
+        a1_col = held.tile([P, 1], F32, name="a1_col")
+        nc.scalar.dma_start(a1_col[:], a1)
+        c1_col = held.tile([P, 1], F32, name="c1_col")
+        nc.scalar.dma_start(c1_col[:], c1)
+
+        cw2_sb = held.tile([P, D], BF16, name="cw2_sb")
+        nc.sync.dma_start(cw2_sb[:], cw2)
+        w_sb = held.tile([P, M], BF16, name="w_sb")
+        nc.sync.dma_start(w_sb[:], w)
+
+        identity = held.tile([P, P], BF16, name="identity")
+        masks.make_identity(nc, identity[:])
+
+        flipped = psum.tile([P, S], BF16, name="flipped")
+        for c in range(S // P):
+            nc.tensor.transpose(flipped[:, c * P : (c + 1) * P], table_rows[:, c, :], identity[:])
+        window = held.tile([P, S], BF16, name="window")
+        nc.vector.tensor_copy(window[:], flipped[:])
+
+        h = held.tile([P, N], BF16, name="h")
+        nc.scalar.activation(h[:], u[:], TANH, bias=c1_col[:], scale=a1_col[:])
+        cont_ps = psum.tile([P, N], F32, name="cont_ps")
+        nc.tensor.matmul(cont_ps[:], cw2_sb[:], h[:], start=True, stop=True)
+        cont = held.tile([P, N], BF16, name="cont")
+        nc.scalar.copy(cont[:], cont_ps[:])
+
+        banks = [psum.tile([P, N], F32, name=f"bank{m}") for m in range(M // P)]
+        for m in range(M // P):
+            nc.tensor.matmul(
+                banks[m][:], w_sb[:, m * P : (m + 1) * P], window[:].indirect(offsets[:]), start=True, stop=False
+            )
+        for m in range(M // P):
+            nc.tensor.matmul(banks[m][:], w_sb[:, m * P : (m + 1) * P], cont[:], start=False, stop=True)
+
+        for m in range(M // P):
+            staged = held.tile([P, N], F32, name=f"staged{m}")
+            if m % 2 == 0:
+                nc.vector.tensor_copy(staged[:], banks[m][:])
+                nc.sync.dma_start(out[m * P : (m + 1) * P, :], staged[:])
+            else:
+                nc.scalar.copy(staged[:], banks[m][:])
+                nc.scalar.dma_start(out[m * P : (m + 1) * P, :], staged[:])

@@ -11,37 +11,42 @@ FLOPS = 2 * D * M * N * 2 + 2 * D * D * N
 
 def tile_strats_kernel(tc, table, w, values, times, a1, c1, cw2, offs, out):
     nc = tc.nc
+    blocks = S // P
+    halves = 2
+    per_half = blocks // halves
     with (
         tc.tile_pool(name="held", bufs=1) as held,
         tc.psum_pool(name="psum", bufs=1) as psum,
     ):
-        offsets = held.tile([P, N // 16], U16, name="offsets")
-        nc.sync.dma_start(offsets[:], offs)
-
-        table_rows = held.tile([P, S // P, D], BF16, name="table_rows")
-        nc.sync.dma_start(table_rows[:], table.rearrange("(c p) d -> p c d", p=P))
+        table_rows = [held.tile([P, per_half, D], BF16, name=f"table_rows{k}") for k in range(halves)]
+        rows_of_half = table.rearrange("(k c p) d -> k p c d", k=halves, p=P)
+        nc.sync.dma_start(table_rows[0][:], rows_of_half[0])
+        nc.scalar.dma_start(table_rows[1][:], rows_of_half[1])
 
         u = held.tile([P, N], F32, name="u")
         nc.scalar.dma_start(u[0:E, :], values.broadcast_to([E, N]))
         nc.scalar.dma_start(u[E:P, :], times.broadcast_to([P - E, N]))
         a1_col = held.tile([P, 1], F32, name="a1_col")
-        nc.scalar.dma_start(a1_col[:], a1)
+        nc.sync.dma_start(a1_col[:], a1)
         c1_col = held.tile([P, 1], F32, name="c1_col")
-        nc.scalar.dma_start(c1_col[:], c1)
+        nc.sync.dma_start(c1_col[:], c1)
 
         cw2_sb = held.tile([P, D], BF16, name="cw2_sb")
         nc.sync.dma_start(cw2_sb[:], cw2)
         w_sb = held.tile([P, M], BF16, name="w_sb")
-        nc.sync.dma_start(w_sb[:], w)
+        nc.scalar.dma_start(w_sb[:], w)
+        offsets = held.tile([P, N // 16], U16, name="offsets")
+        nc.sync.dma_start(offsets[:], offs)
 
         identity = held.tile([P, P], BF16, name="identity")
         masks.make_identity(nc, identity[:])
 
-        flipped = psum.tile([P, S], BF16, name="flipped")
-        for c in range(S // P):
-            nc.tensor.transpose(flipped[:, c * P : (c + 1) * P], table_rows[:, c, :], identity[:])
         window = held.tile([P, S], BF16, name="window")
-        nc.vector.tensor_copy(window[:], flipped[:])
+        for k in range(halves):
+            flipped = psum.tile([P, per_half * P], BF16, name=f"flipped{k}")
+            for c in range(per_half):
+                nc.tensor.transpose(flipped[:, c * P : (c + 1) * P], table_rows[k][:, c, :], identity[:])
+            nc.vector.tensor_copy(window[:, k * per_half * P : (k + 1) * per_half * P], flipped[:])
 
         h = held.tile([P, N], BF16, name="h")
         nc.scalar.activation(h[:], u[:], TANH, bias=c1_col[:], scale=a1_col[:])

@@ -50,7 +50,7 @@ def tile_strats_kernel(tc, table, w, values, times, a1, c1, cw2, offs, out):
 
         h = held.tile([P, N], BF16, name="h")
         nc.scalar.activation(h[:], u[:], TANH, bias=c1_col[:], scale=a1_col[:])
-        cont_ps = psum.tile([P, N], F32, name="cont_ps")
+        cont_ps = psum.tile([P, N], F32, name="cont_ps", tag="flipped0")
         nc.tensor.matmul(cont_ps[:], cw2_sb[:], h[:], start=True, stop=True)
         cont = held.tile([P, N], BF16, name="cont")
         nc.scalar.copy(cont[:], cont_ps[:])

@@ -41,6 +41,10 @@ def tile_strats_kernel(tc, table, w, values, times, a1, c1, cw2, offs, out):
         identity = held.tile([P, P], BF16, name="identity")
         masks.make_identity(nc, identity[:])
 
+        scratch = held.tile([P, 1], F32, name="scratch")
+        nc.vector.memset(scratch[:], 0.0)
+        nc.scalar.activation(scratch[:], scratch[:], TANH)
+
         window = held.tile([P, S], BF16, name="window")
         for k in range(halves):
             flipped = psum.tile([P, per_half * P], BF16, name=f"flipped{k}")

@@ -5,6 +5,7 @@ P = 128
 S, D, M, N, E = 512, 128, 512, 256, 64
 BF16, F32, U16 = mybir.dt.bfloat16, mybir.dt.float32, mybir.dt.uint16
 TANH = mybir.ActivationFunctionType.Tanh
+ADD = mybir.AluOpType.add
 
 FLOPS = 2 * D * M * N * 2 + 2 * D * D * N
 
@@ -59,19 +60,23 @@ def tile_strats_kernel(tc, table, w, values, times, a1, c1, cw2, offs, out):
         cont = held.tile([P, N], BF16, name="cont")
         nc.scalar.copy(cont[:], cont_ps[:])
 
-        banks = [psum.tile([P, N], F32, name=f"bank{m}") for m in range(M // P)]
-        for m in range(M // P):
+        blocks_out = M // P
+        last = blocks_out - 1
+        banks = [psum.tile([P, N], F32, name=f"bank{m}") for m in range(blocks_out)]
+        for m in range(blocks_out):
             nc.tensor.matmul(
-                banks[m][:], w_sb[:, m * P : (m + 1) * P], window[:].indirect(offsets[:]), start=True, stop=False
+                banks[m][:], w_sb[:, m * P : (m + 1) * P], window[:].indirect(offsets[:]), start=True, stop=(m == last)
             )
-        for m in range(M // P):
+        for m in range(last):
             nc.tensor.matmul(banks[m][:], w_sb[:, m * P : (m + 1) * P], cont[:], start=False, stop=True)
 
-        for m in range(M // P):
-            staged = held.tile([P, N], F32, name=f"staged{m}")
-            if m % 2 == 0:
-                nc.vector.tensor_copy(staged[:], banks[m][:])
-                nc.sync.dma_start(out[m * P : (m + 1) * P, :], staged[:])
+        staged = [held.tile([P, N], F32, name=f"staged{m}") for m in range(blocks_out)]
+        nc.vector.tensor_tensor(staged[last][:], banks[last][:], cont[:], ADD)
+        nc.sync.dma_start(out[last * P : (last + 1) * P, :], staged[last][:])
+        for m in range(last):
+            if m % 2 == 1:
+                nc.vector.tensor_copy(staged[m][:], banks[m][:])
+                nc.sync.dma_start(out[m * P : (m + 1) * P, :], staged[m][:])
             else:
-                nc.scalar.copy(staged[:], banks[m][:])
-                nc.scalar.dma_start(out[m * P : (m + 1) * P, :], staged[:])
+                nc.scalar.copy(staged[m][:], banks[m][:])
+                nc.scalar.dma_start(out[m * P : (m + 1) * P, :], staged[m][:])

@@ -14,30 +14,29 @@ def tile_strats_kernel(tc, table, w, values, times, a1, c1, cw2, offs, out):
     nc = tc.nc
     blocks = S // P
     halves = 2
-    per_half = blocks // halves
+    half = N // halves
     with (
         tc.tile_pool(name="held", bufs=1) as held,
         tc.psum_pool(name="psum", bufs=1) as psum,
     ):
-        table_rows = [held.tile([P, per_half, D], BF16, name=f"table_rows{k}") for k in range(halves)]
-        rows_of_half = table.rearrange("(k c p) d -> k p c d", k=halves, p=P)
-        nc.sync.dma_start(table_rows[0][:], rows_of_half[0])
-        nc.scalar.dma_start(table_rows[1][:], rows_of_half[1])
+        table_rows = [held.tile([P, D], BF16, name=f"table_rows{b}") for b in range(blocks)]
+        for b in range(blocks):
+            nc.sync.dma_start(table_rows[b][:], table[b * P : (b + 1) * P, :])
 
         u = held.tile([P, N], F32, name="u")
-        nc.scalar.dma_start(u[0:E, :], values.broadcast_to([E, N]))
-        nc.scalar.dma_start(u[E:P, :], times.broadcast_to([P - E, N]))
+        nc.sync.dma_start(u[0:E, :], values.broadcast_to([E, N]))
+        nc.sync.dma_start(u[E:P, :], times.broadcast_to([P - E, N]))
         a1_col = held.tile([P, 1], F32, name="a1_col")
-        nc.sync.dma_start(a1_col[:], a1)
+        nc.scalar.dma_start(a1_col[:], a1)
         c1_col = held.tile([P, 1], F32, name="c1_col")
-        nc.sync.dma_start(c1_col[:], c1)
+        nc.scalar.dma_start(c1_col[:], c1)
 
         cw2_sb = held.tile([P, D], BF16, name="cw2_sb")
         nc.sync.dma_start(cw2_sb[:], cw2)
-        w_sb = held.tile([P, M], BF16, name="w_sb")
-        nc.scalar.dma_start(w_sb[:], w)
         offsets = held.tile([P, N // 16], U16, name="offsets")
         nc.sync.dma_start(offsets[:], offs)
+        w_sb = held.tile([P, M], BF16, name="w_sb")
+        nc.sync.dma_start(w_sb[:], w)
 
         identity = held.tile([P, P], BF16, name="identity")
         masks.make_identity(nc, identity[:])
@@ -47,23 +46,24 @@ def tile_strats_kernel(tc, table, w, values, times, a1, c1, cw2, offs, out):
         nc.scalar.activation(scratch[:], scratch[:], TANH)
 
         window = held.tile([P, S], BF16, name="window")
-        for k in range(halves):
-            flipped = psum.tile([P, per_half * P], BF16, name=f"flipped{k}")
-            for c in range(per_half):
-                nc.tensor.transpose(flipped[:, c * P : (c + 1) * P], table_rows[k][:, c, :], identity[:])
-            nc.vector.tensor_copy(window[:, k * per_half * P : (k + 1) * per_half * P], flipped[:])
+        for b in range(blocks):
+            flipped = psum.tile([P, P], BF16, name=f"flipped{b}")
+            nc.tensor.transpose(flipped[:], table_rows[b][:], identity[:])
+            nc.vector.tensor_copy(window[:, b * P : (b + 1) * P], flipped[:])
 
         h = held.tile([P, N], BF16, name="h")
-        nc.scalar.activation(h[:], u[:], TANH, bias=c1_col[:], scale=a1_col[:])
         cont_ps = psum.tile([P, N], F32, name="cont_ps", tag="flipped0")
-        nc.tensor.matmul(cont_ps[:], cw2_sb[:], h[:], start=True, stop=True)
+        for k in range(halves):
+            cols = slice(k * half, (k + 1) * half)
+            nc.scalar.activation(h[:, cols], u[:, cols], TANH, bias=c1_col[:], scale=a1_col[:])
+            nc.tensor.matmul(cont_ps[:, cols], cw2_sb[:], h[:, cols], start=True, stop=True)
         cont = held.tile([P, N], BF16, name="cont")
         nc.scalar.copy(cont[:], cont_ps[:])
 
         blocks_out = M // P
         last = blocks_out - 1
         banks = [psum.tile([P, N], F32, name=f"bank{m}") for m in range(blocks_out)]
-        for m in range(blocks_out):
+        for m in [last] + list(range(last)):
             nc.tensor.matmul(
                 banks[m][:], w_sb[:, m * P : (m + 1) * P], window[:].indirect(offsets[:]), start=True, stop=(m == last)
             )
@@ -74,7 +74,7 @@ def tile_strats_kernel(tc, table, w, values, times, a1, c1, cw2, offs, out):
         nc.vector.tensor_tensor(staged[last][:], banks[last][:], cont[:], ADD)
         nc.sync.dma_start(out[last * P : (last + 1) * P, :], staged[last][:])
         for m in range(last):
-            if m % 2 == 1:
+            if m % 2 == 0:
                 nc.vector.tensor_copy(staged[m][:], banks[m][:])
                 nc.sync.dma_start(out[m * P : (m + 1) * P, :], staged[m][:])
             else:

@@ -25,11 +25,11 @@ def tile_strats_kernel(tc, table, w, values, times, a1, c1, cw2, offs, out):
 
         u = held.tile([P, N], F32, name="u")
         nc.sync.dma_start(u[0:E, :], values.broadcast_to([E, N]))
-        nc.sync.dma_start(u[E:P, :], times.broadcast_to([P - E, N]))
         a1_col = held.tile([P, 1], F32, name="a1_col")
         nc.scalar.dma_start(a1_col[:], a1)
         c1_col = held.tile([P, 1], F32, name="c1_col")
         nc.scalar.dma_start(c1_col[:], c1)
+        nc.scalar.dma_start(u[E:P, :], times.broadcast_to([P - E, N]))
 
         cw2_sb = held.tile([P, D], BF16, name="cw2_sb")
         nc.sync.dma_start(cw2_sb[:], cw2)

@@ -14,29 +14,31 @@ def tile_strats_kernel(tc, table, w, values, times, a1, c1, cw2, offs, out):
     nc = tc.nc
     blocks = S // P
     halves = 2
+    per_half = blocks // halves
     half = N // halves
     with (
         tc.tile_pool(name="held", bufs=1) as held,
         tc.psum_pool(name="psum", bufs=1) as psum,
     ):
-        table_rows = [held.tile([P, D], BF16, name=f"table_rows{b}") for b in range(blocks)]
-        for b in range(blocks):
-            nc.sync.dma_start(table_rows[b][:], table[b * P : (b + 1) * P, :])
+        table_rows = [held.tile([P, per_half, D], BF16, name=f"table_rows{k}") for k in range(halves)]
+        rows_of_half = table.rearrange("(k c p) d -> k p c d", k=halves, p=P)
+        for k in range(halves):
+            nc.sync.dma_start(table_rows[k][:], rows_of_half[k])
 
         u = held.tile([P, N], F32, name="u")
         nc.sync.dma_start(u[0:E, :], values.broadcast_to([E, N]))
-        a1_col = held.tile([P, 1], F32, name="a1_col")
-        nc.scalar.dma_start(a1_col[:], a1)
-        c1_col = held.tile([P, 1], F32, name="c1_col")
-        nc.scalar.dma_start(c1_col[:], c1)
         nc.scalar.dma_start(u[E:P, :], times.broadcast_to([P - E, N]))
+        a1_col = held.tile([P, 1], F32, name="a1_col")
+        nc.sync.dma_start(a1_col[:], a1)
+        c1_col = held.tile([P, 1], F32, name="c1_col")
+        nc.sync.dma_start(c1_col[:], c1)
 
         cw2_sb = held.tile([P, D], BF16, name="cw2_sb")
         nc.sync.dma_start(cw2_sb[:], cw2)
         offsets = held.tile([P, N // 16], U16, name="offsets")
         nc.sync.dma_start(offsets[:], offs)
-        w_sb = held.tile([P, M], BF16, name="w_sb")
-        nc.sync.dma_start(w_sb[:], w)
+        w_sb = held.tile([P, M - P], BF16, name="w_sb")
+        nc.sync.dma_start(w_sb[:], w[:, 0 : M - P])
 
         identity = held.tile([P, P], BF16, name="identity")
         masks.make_identity(nc, identity[:])
@@ -48,7 +50,7 @@ def tile_strats_kernel(tc, table, w, values, times, a1, c1, cw2, offs, out):
         window = held.tile([P, S], BF16, name="window")
         for b in range(blocks):
             flipped = psum.tile([P, P], BF16, name=f"flipped{b}")
-            nc.tensor.transpose(flipped[:], table_rows[b][:], identity[:])
+            nc.tensor.transpose(flipped[:], table_rows[b // per_half][:, b % per_half, :], identity[:])
             nc.vector.tensor_copy(window[:, b * P : (b + 1) * P], flipped[:])
 
         h = held.tile([P, N], BF16, name="h")
@@ -63,9 +65,10 @@ def tile_strats_kernel(tc, table, w, values, times, a1, c1, cw2, offs, out):
         blocks_out = M // P
         last = blocks_out - 1
         banks = [psum.tile([P, N], F32, name=f"bank{m}") for m in range(blocks_out)]
-        for m in [last] + list(range(last)):
+        nc.tensor.matmul(banks[last][:], identity[:], window[:].indirect(offsets[:]), start=True, stop=True)
+        for m in range(last):
             nc.tensor.matmul(
-                banks[m][:], w_sb[:, m * P : (m + 1) * P], window[:].indirect(offsets[:]), start=True, stop=(m == last)
+                banks[m][:], w_sb[:, m * P : (m + 1) * P], window[:].indirect(offsets[:]), start=True, stop=False
             )
         for m in range(last):
             nc.tensor.matmul(banks[m][:], w_sb[:, m * P : (m + 1) * P], cont[:], start=False, stop=True)

@@ -79,7 +79,6 @@ def tile_strats_kernel(tc, table, w, values, times, a1, c1, cw2, offs, out):
         for m in range(last):
             if m % 2 == 0:
                 nc.vector.tensor_copy(staged[m][:], banks[m][:])
-                nc.sync.dma_start(out[m * P : (m + 1) * P, :], staged[m][:])
             else:
                 nc.scalar.copy(staged[m][:], banks[m][:])
-                nc.scalar.dma_start(out[m * P : (m + 1) * P, :], staged[m][:])
+            nc.sync.dma_start(out[m * P : (m + 1) * P, :], staged[m][:])

@@ -54,13 +54,13 @@ def tile_strats_kernel(tc, table, w, values, times, a1, c1, cw2, offs, out):
             nc.vector.tensor_copy(window[:, b * P : (b + 1) * P], flipped[:])
 
         h = held.tile([P, N], BF16, name="h")
-        cont_ps = psum.tile([P, N], F32, name="cont_ps", tag="flipped0")
+        cont = held.tile([P, N], BF16, name="cont")
         for k in range(halves):
             cols = slice(k * half, (k + 1) * half)
             nc.scalar.activation(h[:, cols], u[:, cols], TANH, bias=c1_col[:], scale=a1_col[:])
-            nc.tensor.matmul(cont_ps[:, cols], cw2_sb[:], h[:, cols], start=True, stop=True)
-        cont = held.tile([P, N], BF16, name="cont")
-        nc.scalar.copy(cont[:], cont_ps[:])
+            cont_ps = psum.tile([P, half], BF16, name=f"cont_ps{k}", tag=f"flipped{k}")
+            nc.tensor.matmul(cont_ps[:], cw2_sb[:], h[:, cols], start=True, stop=True)
+            nc.vector.tensor_copy(cont[:, cols], cont_ps[:])
 
         blocks_out = M // P
         last = blocks_out - 1

@@ -26,12 +26,12 @@ def tile_strats_kernel(tc, table, w, values, times, a1, c1, cw2, offs, out):
             nc.sync.dma_start(table_rows[k][:], rows_of_half[k])
 
         u = held.tile([P, N], F32, name="u")
-        nc.sync.dma_start(u[0:E, :], values.broadcast_to([E, N]))
         nc.scalar.dma_start(u[E:P, :], times.broadcast_to([P - E, N]))
         a1_col = held.tile([P, 1], F32, name="a1_col")
         nc.sync.dma_start(a1_col[:], a1)
         c1_col = held.tile([P, 1], F32, name="c1_col")
         nc.sync.dma_start(c1_col[:], c1)
+        nc.sync.dma_start(u[0:E, :], values.broadcast_to([E, N]))
 
         cw2_sb = held.tile([P, D], BF16, name="cw2_sb")
         nc.sync.dma_start(cw2_sb[:], cw2)

import concourse.masks as masks
import concourse.mybir as mybir

P = 128
S, D, M, N, E = 512, 128, 512, 256, 64
BF16, F32, U16 = mybir.dt.bfloat16, mybir.dt.float32, mybir.dt.uint16
TANH = mybir.ActivationFunctionType.Tanh
ADD = mybir.AluOpType.add

FLOPS = 2 * D * M * N * 2 + 2 * D * D * N


def tile_strats_kernel(tc, table, w, values, times, a1, c1, cw2, offs, out):
    nc = tc.nc
    blocks = S // P
    halves = 2
    per_half = blocks // halves
    half = N // halves
    with (
        tc.tile_pool(name="held", bufs=1) as held,
        tc.psum_pool(name="psum", bufs=1) as psum,
    ):
        table_rows = [held.tile([P, per_half, D], BF16, name=f"table_rows{k}") for k in range(halves)]
        rows_of_half = table.rearrange("(k c p) d -> k p c d", k=halves, p=P)
        for k in range(halves):
            nc.sync.dma_start(table_rows[k][:], rows_of_half[k])

        u = held.tile([P, N], F32, name="u")
        nc.scalar.dma_start(u[E:P, :], times.broadcast_to([P - E, N]))
        a1_col = held.tile([P, 1], F32, name="a1_col")
        nc.sync.dma_start(a1_col[:], a1)
        c1_col = held.tile([P, 1], F32, name="c1_col")
        nc.sync.dma_start(c1_col[:], c1)
        nc.sync.dma_start(u[0:E, :], values.broadcast_to([E, N]))

        cw2_sb = held.tile([P, D], BF16, name="cw2_sb")
        nc.sync.dma_start(cw2_sb[:], cw2)
        offsets = held.tile([P, N // 16], U16, name="offsets")
        nc.sync.dma_start(offsets[:], offs)
        w_sb = held.tile([P, M - P], BF16, name="w_sb")
        nc.sync.dma_start(w_sb[:], w[:, 0 : M - P])

        identity = held.tile([P, P], BF16, name="identity")
        masks.make_identity(nc, identity[:])

        scratch = held.tile([P, 1], F32, name="scratch")
        nc.vector.memset(scratch[:], 0.0)
        nc.scalar.activation(scratch[:], scratch[:], TANH)

        window = held.tile([P, S], BF16, name="window")
        for b in range(blocks):
            flipped = psum.tile([P, P], BF16, name=f"flipped{b}")
            nc.tensor.transpose(flipped[:], table_rows[b // per_half][:, b % per_half, :], identity[:])
            nc.vector.tensor_copy(window[:, b * P : (b + 1) * P], flipped[:])

        h = held.tile([P, N], BF16, name="h")
        cont = held.tile([P, N], BF16, name="cont")
        for k in range(halves):
            cols = slice(k * half, (k + 1) * half)
            nc.scalar.activation(h[:, cols], u[:, cols], TANH, bias=c1_col[:], scale=a1_col[:])
            cont_ps = psum.tile([P, half], BF16, name=f"cont_ps{k}", tag=f"flipped{k}")
            nc.tensor.matmul(cont_ps[:], cw2_sb[:], h[:, cols], start=True, stop=True)
            nc.vector.tensor_copy(cont[:, cols], cont_ps[:])

        blocks_out = M // P
        last = blocks_out - 1
        banks = [psum.tile([P, N], F32, name=f"bank{m}") for m in range(blocks_out)]
        nc.tensor.matmul(banks[last][:], identity[:], window[:].indirect(offsets[:]), start=True, stop=True)
        for m in range(last):
            nc.tensor.matmul(
                banks[m][:], w_sb[:, m * P : (m + 1) * P], window[:].indirect(offsets[:]), start=True, stop=False
            )
        for m in range(last):
            nc.tensor.matmul(banks[m][:], w_sb[:, m * P : (m + 1) * P], cont[:], start=False, stop=True)

        staged = [held.tile([P, N], F32, name=f"staged{m}") for m in range(blocks_out)]
        nc.vector.tensor_tensor(staged[last][:], banks[last][:], cont[:], ADD)
        nc.sync.dma_start(out[last * P : (last + 1) * P, :], staged[last][:])
        for m in range(last):
            if m % 2 == 0:
                nc.vector.tensor_copy(staged[m][:], banks[m][:])
            else:
                nc.scalar.copy(staged[m][:], banks[m][:])
            nc.sync.dma_start(out[m * P : (m + 1) * P, :], staged[m][:])
